import numpy as np
import ml_dtypes


def mxq(x, axis, fmt="e4m3"):
    dtype, down = {"e4m3": (ml_dtypes.float8_e4m3fn, 7), "e5m2": (ml_dtypes.float8_e5m2, 14)}[fmt]
    v = np.moveaxis(np.asarray(x, np.float32).astype(ml_dtypes.bfloat16).astype(np.float64), axis, -1)
    blocks = v.reshape(v.shape[:-1] + (-1, 32))
    amax = np.abs(blocks).max(-1, keepdims=True)
    byte = np.maximum(np.where(amax > 0, np.frexp(amax)[1] - 1 + 127, 0) - down, 1)
    scale = np.exp2(byte - 127.0)
    codes = (blocks / scale).astype(np.float32).astype(dtype).astype(np.float64)
    return np.moveaxis((codes * scale).reshape(v.shape), -1, axis)


WIDE = False


def mx_kscale(k):
    if not WIDE:
        return np.ones(k)
    levels = np.array([10, -10, 5, -5, 0])
    if k % 512:
        return np.exp2(np.random.permutation(np.resize(levels, k // 32))).repeat(32)
    a = np.empty((k // 512, 16))
    for p in range(k // 512):
        a[p, :8] = np.random.permutation(np.resize(levels, 8))
        for g in range(8):
            far = levels[np.abs(levels - a[p, g]) >= 10]
            a[p, g + 8] = far[np.random.randint(len(far))]
    return np.exp2(a.ravel()).repeat(32)


BF16 = ml_dtypes.bfloat16


def bf(x):
    return np.asarray(x, np.float32).astype(BF16)


def f64(x):
    return np.asarray(x).astype(np.float64)


E2M1 = np.array([0.0, 0.5, 1.0, 1.5, 2.0, 3.0, 4.0, 6.0, -0.0, -0.5, -1.0, -1.5, -2.0, -3.0, -4.0, -6.0])


def pack_weight(w, fmt):
    k, n = w.shape
    w = f64(bf(w)).reshape(k // 32, 32, n)
    amax = np.abs(w).max(1)
    if fmt == "e4m3":
        byte = np.frexp(amax)[1] - 1 + 127 - 7
    else:
        mant, ex = np.frexp(amax / 6.0)
        byte = np.where(mant > 0.5, ex, ex - 1) + 127
    byte = np.clip(np.where(amax > 0, byte, 1), 1, 254)
    scaled = (w * np.exp2(127.0 - byte)[:, None, :]).reshape(k, n).astype(np.float32)
    by_word = np.ascontiguousarray(scaled.reshape(k // 512, 128, 4, n).transpose(0, 1, 3, 2))
    if fmt == "e4m3":
        words = by_word.astype(ml_dtypes.float8_e4m3fn).view(np.uint8)
    else:
        c = by_word.astype(ml_dtypes.float4_e2m1fn).view(np.uint8) & 0xF
        words = c[..., 0::2] | (c[..., 1::2] << 4)
    return np.ascontiguousarray(words), np.ascontiguousarray(byte.astype(np.uint8).reshape(k // 512, 16, n))


def unpack_weight(words, scales, fmt):
    g, p, n, _ = words.shape
    if fmt == "e4m3":
        vals = np.ascontiguousarray(words).view(ml_dtypes.float8_e4m3fn).astype(np.float64)
    else:
        nib = np.empty((g, p, n, 4), np.uint8)
        nib[..., 0::2] = words & 0xF
        nib[..., 1::2] = words >> 4
        vals = E2M1[nib]
    vals = vals * np.repeat(np.exp2(scales.astype(np.float64) - 127.0), 8, axis=1)[..., None]
    return vals.transpose(0, 1, 3, 2).reshape(g * 512, n)


B, T, N, D, H, F = 2, 512, 4, 512, 8, 1024
S = B * N
EPS = 1e-5


def layernorm(v, g, b):
    mu = v.mean(-1, keepdims=True)
    var = np.square(v - mu).mean(-1, keepdims=True)
    return (v - mu) / np.sqrt(var + EPS) * g + b


def draw0():
    s = mx_kscale(D)
    t = mx_kscale(D)
    ax_cat = bf(np.random.standard_normal((S, T, D)) * 4.0 * s)
    features = bf(np.random.standard_normal((B, T, N, D)))
    wout_w = np.random.standard_normal((D, D)) * 0.5 / np.sqrt(D) / s
    wout_w_words, wout_w_scales = pack_weight(wout_w.T, "e4m3")
    ln_g = bf((1.0 + 0.1 * np.random.standard_normal(D)) * t)
    ln_b = bf(0.1 * np.random.standard_normal(D) * t)
    ff1_w = np.random.standard_normal((F, D)) / np.sqrt(D) / t
    ff1_w_words, ff1_w_scales = pack_weight(ff1_w.T, "e4m3")
    return {"ax_cat": ax_cat,
            "features": features,
            "wout_w_words": wout_w_words,
            "wout_w_scales": wout_w_scales,
            "ln_g": ln_g,
            "ln_b": ln_b,
            "ff1_w_words": ff1_w_words,
            "ff1_w_scales": ff1_w_scales,
            "ff1_b": bf(0.1 * np.random.standard_normal(F))}


def core(ax_cat, features, wout_w_words, wout_w_scales, ln_g, ln_b, ff1_w_words, ff1_w_scales, ff1_b):
    x = f64(features).transpose(0, 2, 1, 3).reshape(S, T, D)
    y = mxq(f64(ax_cat), 2, "e4m3") @ unpack_weight(wout_w_words, wout_w_scales, "e4m3")
    m = layernorm(y + x, f64(ln_g), f64(ln_b))
    return np.maximum((mxq(m, 2, "e4m3") @ unpack_weight(ff1_w_words, ff1_w_scales, "e4m3")) + f64(ff1_b), 0.0)


def e4m3fn_bytes(y):
    return np.clip(np.asarray(y, np.float64), -448.0, 448.0).astype(np.float32).astype(ml_dtypes.float8_e4m3fn).view(np.uint8)


def e4m3fn_values(b):
    return np.asarray(b, np.uint8).view(ml_dtypes.float8_e4m3fn).astype(np.float64)


def setup_inputs():
    d = draw0()
    x0 = np.asarray(d['ax_cat']).astype(np.float64)
    s = (np.max(np.abs(x0), axis=(0, 1), keepdims=True) / 448.0).astype(np.float32)
    out = {}
    for k, v in d.items():
        if k == 'ax_cat':
            out['ax_cat_bytes'] = e4m3fn_bytes(x0 / s.astype(np.float64))
            out['ax_cat_scale'] = s
        else:
            out[k] = v
    return out


def reference(ax_cat_bytes, ax_cat_scale, features, wout_w_words, wout_w_scales, ln_g, ln_b, ff1_w_words, ff1_w_scales, ff1_b):
    return core(e4m3fn_values(ax_cat_bytes) * ax_cat_scale.astype(np.float64), features, wout_w_words, wout_w_scales, ln_g, ln_b, ff1_w_words, ff1_w_scales, ff1_b)

@@ -1,0 +1,322 @@
+from contextlib import ExitStack
+
+import concourse.mybir as mybir
+from concourse.masks import make_identity
+
+SEQS, T_LEN, D, F = 8, 512, 512, 1024
+NODES = 4
+EPS = 1e-5
+FLOPS = 2 * SEQS * T_LEN * D * (D + F)
+
+F32 = mybir.dt.float32
+BF16 = mybir.dt.bfloat16
+U32 = mybir.dt.uint32
+I32 = mybir.dt.int32
+U8 = mybir.dt.uint8
+FP8 = mybir.dt.float8_e4m3fn
+FP8X4 = mybir.dt.float8_e4m3fn_x4
+ADD = mybir.AluOpType.add
+MULT = mybir.AluOpType.mult
+MAX = mybir.AluOpType.max
+POW = mybir.AluOpType.pow
+ACT = mybir.ActivationFunctionType
+
+P = 128
+PACK = 4
+ROWS = T_LEN // P
+PAIR = 2
+PAIRS = SEQS * ROWS // PAIR
+
+STEP = (
+    ("store", 8),
+    ("square", 3),
+    ("z10", 7),
+    ("resid", 2),
+    ("weave", 5),
+    ("relu0", 7),
+    ("turn", 1),
+    ("mean", 2),
+    ("norm", 3),
+    ("gather", 1),
+    ("quant1", 1),
+    ("z00", 6),
+    ("z01", 6),
+    ("quant2", 5),
+    ("relu1", 7),
+    ("turn2", 4),
+    ("scale", 0),
+    ("z11", 6),
+    ("mm1", 1),
+    ("affine", 4),
+)
+
+
+def tile_temporalatt_pb_t_w8_kernel(
+    tc, ax_cat_bytes, ax_cat_scale, features, wout_w_words, wout_w_scales,
+    ln_g, ln_b, ff1_w_words, ff1_w_scales, ff1_b, out,
+):
+    nc = tc.nc
+    with ExitStack() as ctx:
+        keep = ctx.enter_context(tc.tile_pool(name="keep", bufs=1))
+        work = ctx.enter_context(tc.tile_pool(name="work", bufs=3))
+        small = ctx.enter_context(tc.tile_pool(name="small", bufs=6))
+        psum2 = ctx.enter_context(tc.psum_pool(name="psum2", bufs=2))
+        psum1 = ctx.enter_context(tc.psum_pool(name="psum1", bufs=1))
+        ctx.enter_context(tc.manual_schedule())
+
+        scale2 = keep.tile([P, PAIR, D], F32, name="scale2")
+        nc.scalar.dma_start(out=scale2[:, 0, :], in_=ax_cat_scale.rearrange("a o k -> (a o k)").partition_broadcast(P))
+
+        w1s_raw = keep.tile([P, D], U8, name="w1s_raw", align_bytes=64)
+        w2s = keep.tile([P, F], U8, name="w2s", align_bytes=64)
+        nc.vector.memset(w1s_raw[:].bitcast(I32), 0)
+        nc.vector.memset(w2s[:].bitcast(I32), 0)
+
+        ax = [None] * SEQS
+
+        def load_ax(s):
+            ax[s] = keep.tile([P, ROWS * D], U8, name=f"ax{s}", align_bytes=64)
+            nc.sync.dma_start(out=ax[s][:], in_=ax_cat_bytes[s].rearrange("(p j) k -> p (j k)", j=ROWS))
+
+        feat = {}
+
+        def load_feat(b, j):
+            feat[b, j] = keep.tile([P, NODES, D], BF16, name=f"feat{b}_{j}")
+            nc.sync.dma_start(
+                out=feat[b, j][:],
+                in_=features[b].rearrange("(p j) n d -> p j n d", j=ROWS)[:, j, :, :],
+            )
+
+        load_ax(0)
+        w1_raw = keep.tile([P, D], U32, name="w1_raw", align_bytes=64)
+        for r in range(4):
+            nc.sync.dma_start(out=w1s_raw[r:P:32, :].bitcast(I32), in_=wout_w_scales[0][r:16:4, :].bitcast(I32))
+        nc.sync.dma_start(out=w1_raw[:].bitcast(I32), in_=wout_w_words[0].rearrange("p n t -> p (n t)").bitcast(I32))
+        load_feat(0, 0)
+        load_feat(0, 1)
+        gb_bf = keep.tile([P, 2, 16], BF16, name="gb_bf")
+        nc.scalar.dma_start(out=gb_bf[:, 0, :PACK], in_=ln_g.rearrange("(p t) -> p t", t=PACK))
+        nc.scalar.dma_start(out=gb_bf[:, 1, :PACK], in_=ln_b.rearrange("(p t) -> p t", t=PACK))
+        load_feat(0, 2)
+        load_feat(0, 3)
+        load_ax(1)
+        w2 = keep.tile([P, F], U32, name="w2", align_bytes=64)
+        nc.sync.dma_start(out=w2[:].bitcast(I32), in_=ff1_w_words[0].rearrange("p n t -> p (n t)").bitcast(I32))
+        for r in range(4):
+            nc.sync.dma_start(out=w2s[r:P:32, :].bitcast(I32), in_=ff1_w_scales[0][r:16:4, :].bitcast(I32))
+        bias = keep.tile([P, F], BF16, name="bias")
+        nc.sync.dma_start(out=bias[:], in_=ff1_b.partition_broadcast(P))
+        load_ax(2)
+        load_ax(3)
+        for j in range(ROWS):
+            load_feat(1, j)
+        for s in range(4, SEQS):
+            load_ax(s)
+
+        ident = keep.tile([P, P], F32, name="ident")
+        make_identity(nc, ident[:])
+        half = keep.tile([P, PAIR], F32, name="half")
+        nc.gpsimd.memset(half[:], -0.5)
+        warm = keep.tile([P, 1], F32, name="warm")
+        nc.gpsimd.memset(warm[:], 0.0)
+        nc.scalar.activation(out=warm[:], in_=warm[:], func=ACT.Square)
+        nc.vector.tensor_copy(out=scale2[:, 1, :], in_=scale2[:, 0, :])
+        gb = keep.tile([P, 2, PACK], F32, name="gb")
+        w1 = keep.tile([P, D], U32, name="w1", align_bytes=64)
+        w1s = keep.tile([P, D], U8, name="w1s", align_bytes=64)
+
+        def prepare_weights():
+            nc.vector.tensor_copy(
+                out=w1[:].bitcast(I32).rearrange("p (t m) -> p t m", t=PACK),
+                in_=w1_raw[:].bitcast(I32).rearrange("p (m t) -> p t m", t=PACK),
+            )
+            nc.vector.tensor_copy(
+                out=w1s[:].rearrange("p (t m) -> p t m", t=PACK),
+                in_=w1s_raw[:].rearrange("p (m t) -> p t m", t=PACK),
+            )
+            nc.vector.tensor_copy(out=gb[:], in_=gb_bf[:, :, :PACK])
+
+        st = [dict() for unused in range(PAIRS)]
+
+        def scale(i):
+            s, h = divmod(i, ROWS // PAIR)
+            a = work.tile([P, PAIR, D], BF16, name="a")
+            nc.vector.tensor_tensor(
+                out=a[:].rearrange("p j k -> p (j k)"),
+                in0=ax[s][:, h * PAIR * D:(h + 1) * PAIR * D].bitcast(FP8),
+                in1=scale2[:].rearrange("p j k -> p (j k)"),
+                op=MULT,
+            )
+            st[i]["a"] = a
+
+        def turn(i):
+            xt = psum2.tile([P, PAIR, 2, P], F32, name="xt")
+            words = st[i]["a"][:].rearrange("p j k -> p (j k)").bitcast(F32)
+            for j in range(PAIR):
+                for u in range(2):
+                    nc.tensor.transpose(xt[:, j, u, :], words[:, j * 256 + u:(j + 1) * 256:2], ident[:])
+            st[i]["xt"] = xt
+
+        def gather(i):
+            xg = work.tile([P, PAIR * P * PACK], BF16, name="xg", align_bytes=64)
+            nc.scalar.copy(
+                out=xg[:].bitcast(F32).rearrange("p (j r u) -> p j r u", j=PAIR, u=2),
+                in_=st[i]["xt"][:].rearrange("p j u r -> p j r u"),
+            )
+            st[i]["xg"] = xg
+
+        def quant1(i):
+            xq = work.tile([P, PAIR * P], U32, name="xq", align_bytes=64)
+            xs = work.tile([P, PAIR * P], U8, name="xs", align_bytes=64)
+            nc.vector.quantize_mx(out=xq[:].bitcast(FP8X4), scales=xs[:], in_=st[i]["xg"][:])
+            st[i]["xq"] = xq, xs
+
+        def mm1(i):
+            xq, xs = st[i]["xq"]
+            ys = []
+            for j in range(PAIR):
+                c = slice(j * P, (j + 1) * P)
+                y = psum2.tile([P, D], F32, name="y")
+                nc.tensor.matmul_mx(
+                    out=y[:], lhsT=xq[:, c].bitcast(FP8X4), lhsT_scale=xs[:, c],
+                    rhs=w1[:].bitcast(FP8X4), rhs_scale=w1s[:], start=True, stop=True,
+                )
+                ys.append(y)
+            st[i]["y"] = ys
+
+        def resid(i):
+            s, h = divmod(i, ROWS // PAIR)
+            b, n = divmod(s, NODES)
+            rs = []
+            sums = small.tile([P, PAIR], F32, name="sums")
+            for j, y in enumerate(st[i]["y"]):
+                r = work.tile([P, D], F32, name=f"r{j}")
+                nc.vector.scalar_tensor_tensor(
+                    out=r[:].rearrange("p (t m) -> p t m", t=PACK),
+                    in0=y[:].rearrange("p (t m) -> p t m", t=PACK), scalar=1.0,
+                    in1=feat[b, h * PAIR + j][:, n, :].rearrange("p (m t) -> p t m", t=PACK),
+                    op0=MULT, op1=ADD, accum_out=sums[:, j:j + 1],
+                )
+                rs.append(r)
+            st[i]["r"] = rs
+            st[i]["sums"] = sums
+
+        def mean(i):
+            nm = small.tile([P, PAIR], F32, name="nm")
+            nc.gpsimd.tensor_scalar(out=nm[:], in0=st[i]["sums"][:], scalar1=-1.0 / D, scalar2=0.0, op0=MULT, op1=ADD)
+            st[i]["nm"] = nm
+
+        def square(i):
+            ssq = small.tile([P, PAIR], F32, name="ssq")
+            for j in range(PAIR):
+                sq = work.tile([P, D], BF16, name="sq")
+                nc.scalar.activation(
+                    out=sq[:], in_=st[i]["r"][j][:], func=ACT.Square,
+                    bias=st[i]["nm"][:, j:j + 1], accum_out=ssq[:, j:j + 1],
+                )
+            st[i]["ssq"] = ssq
+
+        def norm(i):
+            var = small.tile([P, PAIR], F32, name="var")
+            rstd = small.tile([P, PAIR], F32, name="rstd")
+            nc.gpsimd.tensor_scalar(out=var[:], in0=st[i]["ssq"][:], scalar1=1.0 / D, scalar2=EPS, op0=MULT, op1=ADD)
+            nc.gpsimd.tensor_tensor(out=rstd[:], in0=var[:], in1=half[:], op=POW)
+            nm = st[i]["nm"]
+            ns = []
+            for j, r in enumerate(st[i]["r"]):
+                nr = work.tile([P, D], F32, name=f"nr{j}")
+                nc.gpsimd.tensor_scalar(
+                    out=nr[:], in0=r[:], scalar1=nm[:, j:j + 1], scalar2=rstd[:, j:j + 1], op0=ADD, op1=MULT,
+                )
+                ns.append(nr)
+            st[i]["n"] = ns
+
+        def turn2(i):
+            ns = st[i]["n"]
+            nts = []
+            for u in range(2):
+                nt = psum1.tile([P, 2, PAIR, P], F32, name=f"nt{u}")
+                for e in range(2):
+                    t = 2 * u + e
+                    for j in range(PAIR):
+                        nc.tensor.transpose(nt[:, e, j, :], ns[j][:, t * P:(t + 1) * P], ident[:])
+                nts.append(nt)
+            st[i]["nt"] = nts
+
+        def affine(i):
+            planes = work.tile([P, PACK, PAIR * P], BF16, name="planes")
+            for u, nt in enumerate(st[i]["nt"]):
+                for e in range(2):
+                    t = 2 * u + e
+                    nc.scalar.activation(
+                        out=planes[:, t, :], in_=nt[:, e, :, :].rearrange("p j r -> p (j r)"), func=ACT.Identity,
+                        scale=gb[:, 0, t:t + 1], bias=gb[:, 1, t:t + 1],
+                    )
+            st[i]["planes"] = planes
+
+        def weave(i):
+            mg = work.tile([P, PAIR * P * PACK], BF16, name="mg", align_bytes=64)
+            copy = nc.scalar.copy if False else nc.vector.tensor_copy
+            copy(
+                out=mg[:].rearrange("p (r t) -> p r t", t=PACK),
+                in_=st[i]["planes"][:].rearrange("p t r -> p r t"),
+            )
+            st[i]["mg"] = mg
+
+        def quant2(i):
+            mq = work.tile([P, PAIR * P], U32, name="mq", align_bytes=64)
+            ms = work.tile([P, PAIR * P], U8, name="ms", align_bytes=64)
+            nc.vector.quantize_mx(out=mq[:].bitcast(FP8X4), scales=ms[:], in_=st[i]["mg"][:])
+            st[i]["mq"] = mq, ms
+            st[i]["o"] = work.tile([P, PAIR, F], F32, name="o")
+
+        def half_out(i, j, h):
+            mq, ms = st[i]["mq"]
+            c = slice(j * P, (j + 1) * P)
+            f = slice(h * 512, (h + 1) * 512)
+            z = psum2.tile([P, 512], F32, name="z")
+            nc.tensor.matmul_mx(
+                out=z[:], lhsT=mq[:, c].bitcast(FP8X4), lhsT_scale=ms[:, c],
+                rhs=w2[:, f].bitcast(FP8X4), rhs_scale=w2s[:, f], start=True, stop=True,
+            )
+            nc.vector.tensor_tensor(out=st[i]["o"][:, j, f], in0=z[:], in1=bias[:, f], op=ADD)
+
+        def relu(i, j):
+            o = st[i]["o"]
+            if False:
+                nc.gpsimd.tensor_scalar(out=o[:, j, :], in0=o[:, j, :], scalar1=0.0, scalar2=0.0, op0=MAX, op1=ADD)
+            else:
+                nc.scalar.activation(out=o[:, j, :], in_=o[:, j, :], func=ACT.Relu)
+            if i == PAIRS - 1:
+                store_token_tile(i, j)
+
+        def store_token_tile(i, j):
+            s, h = divmod(i, ROWS // PAIR)
+            nc.sync.dma_start(
+                out=out[s].rearrange("(p j) f -> p j f", j=ROWS)[:, h * PAIR + j, :], in_=st[i]["o"][:, j, :],
+            )
+
+        def store(i):
+            if i == PAIRS - 1:
+                return
+            s, h = divmod(i, ROWS // PAIR)
+            nc.sync.dma_start(
+                out=out[s].rearrange("(p j) f -> p j f", j=ROWS)[:, h * PAIR:(h + 1) * PAIR, :],
+                in_=st[i]["o"][:],
+            )
+
+        stages = {
+            "scale": scale, "turn": turn, "gather": gather, "quant1": quant1, "mm1": mm1, "resid": resid,
+            "mean": mean, "square": square, "norm": norm, "turn2": turn2, "affine": affine, "weave": weave,
+            "quant2": quant2,
+            "z00": lambda i: half_out(i, 0, 0), "z01": lambda i: half_out(i, 0, 1),
+            "z10": lambda i: half_out(i, 1, 0), "z11": lambda i: half_out(i, 1, 1),
+            "relu0": lambda i: relu(i, 0), "relu1": lambda i: relu(i, 1), "store": store,
+        }
+        deepest = max(lag for name, lag in STEP)
+        for k in range(PAIRS + deepest):
+            for name, lag in STEP:
+                if 0 <= k - lag < PAIRS:
+                    stages[name](k - lag)
+            if k == 0:
+                prepare_weights()

@@ -18,7 +18,6 @@ FP8X4 = mybir.dt.float8_e4m3fn_x4
 ADD = mybir.AluOpType.add
 MULT = mybir.AluOpType.mult
 MAX = mybir.AluOpType.max
-POW = mybir.AluOpType.pow
 ACT = mybir.ActivationFunctionType
 
 P = 128
@@ -28,26 +27,28 @@ PAIR = 2
 PAIRS = SEQS * ROWS // PAIR
 
 STEP = (
-    ("store", 8),
-    ("square", 3),
-    ("z10", 7),
-    ("resid", 2),
-    ("weave", 5),
-    ("relu0", 7),
     ("turn", 1),
-    ("mean", 2),
-    ("norm", 3),
-    ("gather", 1),
-    ("quant1", 1),
-    ("z00", 6),
-    ("z01", 6),
-    ("quant2", 5),
+    ("recip", 3),
     ("relu1", 7),
-    ("turn2", 4),
+    ("resid", 2),
+    ("shift", 3),
+    ("weave", 5),
+    ("quant2", 5),
     ("scale", 0),
-    ("z11", 6),
-    ("mm1", 1),
+    ("turn2", 4),
+    ("store", 7),
+    ("relu0", 6),
+    ("gather", 1),
+    ("mean", 2),
+    ("quant1", 1),
+    ("z01", 5),
     ("affine", 4),
+    ("z00", 5),
+    ("mm1", 1),
+    ("norm", 3),
+    ("z10", 5),
+    ("z11", 5),
+    ("square", 2),
 )
 
 
@@ -115,11 +116,12 @@ def tile_temporalatt_pb_t_w8_kernel(
 
         ident = keep.tile([P, P], F32, name="ident")
         make_identity(nc, ident[:])
-        half = keep.tile([P, PAIR], F32, name="half")
-        nc.gpsimd.memset(half[:], -0.5)
+        zero = keep.tile([P, 1], F32, name="zero")
+        nc.vector.memset(zero[:], 0.0)
+        eps = keep.tile([P, 1], F32, name="eps")
+        nc.vector.tensor_scalar(out=eps[:], in0=zero[:], scalar1=1.0, scalar2=EPS, op0=MULT, op1=ADD)
         warm = keep.tile([P, 1], F32, name="warm")
-        nc.gpsimd.memset(warm[:], 0.0)
-        nc.scalar.activation(out=warm[:], in_=warm[:], func=ACT.Square)
+        nc.scalar.activation(out=warm[:], in_=eps[:], func=ACT.Sqrt)
         nc.vector.tensor_copy(out=scale2[:, 1, :], in_=scale2[:, 0, :])
         gb = keep.tile([P, 2, PACK], F32, name="gb")
         w1 = keep.tile([P, D], U32, name="w1", align_bytes=64)
@@ -203,7 +205,7 @@ def tile_temporalatt_pb_t_w8_kernel(
 
         def mean(i):
             nm = small.tile([P, PAIR], F32, name="nm")
-            nc.gpsimd.tensor_scalar(out=nm[:], in0=st[i]["sums"][:], scalar1=-1.0 / D, scalar2=0.0, op0=MULT, op1=ADD)
+            nc.scalar.activation(out=nm[:], in_=st[i]["sums"][:], func=ACT.Copy, scale=-1.0 / D)
             st[i]["nm"] = nm
 
         def square(i):
@@ -214,19 +216,27 @@ def tile_temporalatt_pb_t_w8_kernel(
                     out=sq[:], in_=st[i]["r"][j][:], func=ACT.Square,
                     bias=st[i]["nm"][:, j:j + 1], accum_out=ssq[:, j:j + 1],
                 )
-            st[i]["ssq"] = ssq
+            std = small.tile([P, PAIR], F32, name="std")
+            nc.scalar.activation(out=std[:], in_=ssq[:], func=ACT.Sqrt, scale=1.0 / D, bias=eps[:])
+            st[i]["std"] = std
+
+        def recip(i):
+            rstd = small.tile([P, PAIR], F32, name="rstd")
+            nc.vector.reciprocal(out=rstd[:], in_=st[i]["std"][:])
+            st[i]["rstd"] = rstd
+
+        def shift(i):
+            nb = small.tile([P, PAIR], F32, name="nb")
+            nc.vector.tensor_tensor(out=nb[:], in0=st[i]["nm"][:], in1=st[i]["rstd"][:], op=MULT)
+            st[i]["nb"] = nb
 
         def norm(i):
-            var = small.tile([P, PAIR], F32, name="var")
-            rstd = small.tile([P, PAIR], F32, name="rstd")
-            nc.gpsimd.tensor_scalar(out=var[:], in0=st[i]["ssq"][:], scalar1=1.0 / D, scalar2=EPS, op0=MULT, op1=ADD)
-            nc.gpsimd.tensor_tensor(out=rstd[:], in0=var[:], in1=half[:], op=POW)
-            nm = st[i]["nm"]
             ns = []
             for j, r in enumerate(st[i]["r"]):
                 nr = work.tile([P, D], F32, name=f"nr{j}")
                 nc.gpsimd.tensor_scalar(
-                    out=nr[:], in0=r[:], scalar1=nm[:, j:j + 1], scalar2=rstd[:, j:j + 1], op0=ADD, op1=MULT,
+                    out=nr[:], in0=r[:], scalar1=st[i]["rstd"][:, j:j + 1], scalar2=st[i]["nb"][:, j:j + 1],
+                    op0=MULT, op1=ADD,
                 )
                 ns.append(nr)
             st[i]["n"] = ns
@@ -256,11 +266,14 @@ def tile_temporalatt_pb_t_w8_kernel(
 
         def weave(i):
             mg = work.tile([P, PAIR * P * PACK], BF16, name="mg", align_bytes=64)
-            copy = nc.scalar.copy if False else nc.vector.tensor_copy
-            copy(
-                out=mg[:].rearrange("p (r t) -> p r t", t=PACK),
-                in_=st[i]["planes"][:].rearrange("p t r -> p r t"),
-            )
+            woven = mg[:].rearrange("p (r t) -> p r t", t=PACK)
+            planes = st[i]["planes"][:].rearrange("p t r -> p r t")
+            if False:
+                nc.scalar.copy(out=woven, in_=planes)
+            elif True:
+                nc.gpsimd.tensor_scalar(out=woven, in0=planes, scalar1=1.0, scalar2=0.0, op0=MULT, op1=ADD)
+            else:
+                nc.vector.tensor_copy(out=woven, in_=planes)
             st[i]["mg"] = mg
 
         def quant2(i):
@@ -283,8 +296,8 @@ def tile_temporalatt_pb_t_w8_kernel(
 
         def relu(i, j):
             o = st[i]["o"]
-            if False:
-                nc.gpsimd.tensor_scalar(out=o[:, j, :], in0=o[:, j, :], scalar1=0.0, scalar2=0.0, op0=MAX, op1=ADD)
+            if i >= 10 and j == 0:
+                nc.vector.tensor_scalar(out=o[:, j, :], in0=o[:, j, :], scalar1=0.0, scalar2=None, op0=MAX)
             else:
                 nc.scalar.activation(out=o[:, j, :], in_=o[:, j, :], func=ACT.Relu)
             if i == PAIRS - 1:
@@ -307,7 +320,7 @@ def tile_temporalatt_pb_t_w8_kernel(
 
         stages = {
             "scale": scale, "turn": turn, "gather": gather, "quant1": quant1, "mm1": mm1, "resid": resid,
-            "mean": mean, "square": square, "norm": norm, "turn2": turn2, "affine": affine, "weave": weave,
+            "mean": mean, "square": square, "recip": recip, "shift": shift, "norm": norm, "turn2": turn2, "affine": affine, "weave": weave,
             "quant2": quant2,
             "z00": lambda i: half_out(i, 0, 0), "z01": lambda i: half_out(i, 0, 1),
             "z10": lambda i: half_out(i, 1, 0), "z11": lambda i: half_out(i, 1, 1),

@@ -27,28 +27,33 @@ PAIR = 2
 PAIRS = SEQS * ROWS // PAIR
 
 STEP = (
-    ("turn", 1),
-    ("recip", 3),
-    ("relu1", 7),
-    ("resid", 2),
     ("shift", 3),
-    ("weave", 5),
-    ("quant2", 5),
-    ("scale", 0),
-    ("turn2", 4),
-    ("store", 7),
-    ("relu0", 6),
-    ("gather", 1),
-    ("mean", 2),
-    ("quant1", 1),
-    ("z01", 5),
+    ("d", 5),
     ("affine", 4),
-    ("z00", 5),
-    ("mm1", 1),
+    ("scale", 0),
+    ("quant2", 5),
     ("norm", 3),
+    ("z01", 6),
+    ("z00", 6),
+    ("d", 1),
+    ("mm1", 1),
+    ("weave", 4),
+    ("resid", 1),
+    ("turn", 0),
+    ("prep", 0),
+    ("d", 0),
+    ("square", 2),
     ("z10", 5),
     ("z11", 5),
-    ("square", 2),
+    ("relu1", 6),
+    ("gather", 0),
+    ("recip", 2),
+    ("store", 7),
+    ("d", 4),
+    ("relu0", 6),
+    ("mean", 1),
+    ("quant1", 0),
+    ("turn2", 3),
 )
 
 
@@ -127,7 +132,9 @@ def tile_temporalatt_pb_t_w8_kernel(
         w1 = keep.tile([P, D], U32, name="w1", align_bytes=64)
         w1s = keep.tile([P, D], U8, name="w1s", align_bytes=64)
 
-        def prepare_weights():
+        def prepare_weights(i):
+            if i > 0:
+                return
             nc.vector.tensor_copy(
                 out=w1[:].bitcast(I32).rearrange("p (t m) -> p t m", t=PACK),
                 in_=w1_raw[:].bitcast(I32).rearrange("p (m t) -> p t m", t=PACK),
@@ -137,6 +144,11 @@ def tile_temporalatt_pb_t_w8_kernel(
                 in_=w1s_raw[:].rearrange("p (m t) -> p t m", t=PACK),
             )
             nc.vector.tensor_copy(out=gb[:], in_=gb_bf[:, :, :PACK])
+
+        junk = psum1.tile([P, P], F32, name="junk")
+
+        def keep_warm(i):
+            nc.tensor.matmul(junk[:], lhsT=ident[:], rhs=ident[:], start=True, stop=True)
 
         st = [dict() for unused in range(PAIRS)]
 
@@ -152,7 +164,7 @@ def tile_temporalatt_pb_t_w8_kernel(
             st[i]["a"] = a
 
         def turn(i):
-            xt = psum2.tile([P, PAIR, 2, P], F32, name="xt")
+            xt = psum1.tile([P, PAIR, 2, P], F32, name="xt")
             words = st[i]["a"][:].rearrange("p j k -> p (j k)").bitcast(F32)
             for j in range(PAIR):
                 for u in range(2):
@@ -234,7 +246,8 @@ def tile_temporalatt_pb_t_w8_kernel(
             ns = []
             for j, r in enumerate(st[i]["r"]):
                 nr = work.tile([P, D], F32, name=f"nr{j}")
-                nc.gpsimd.tensor_scalar(
+                engine = nc.vector if i < 6 else nc.gpsimd
+                engine.tensor_scalar(
                     out=nr[:], in0=r[:], scalar1=st[i]["rstd"][:, j:j + 1], scalar2=st[i]["nb"][:, j:j + 1],
                     op0=MULT, op1=ADD,
                 )
@@ -296,18 +309,19 @@ def tile_temporalatt_pb_t_w8_kernel(
 
         def relu(i, j):
             o = st[i]["o"]
-            if i >= 10 and j == 0:
-                nc.vector.tensor_scalar(out=o[:, j, :], in0=o[:, j, :], scalar1=0.0, scalar2=None, op0=MAX)
-            else:
-                nc.scalar.activation(out=o[:, j, :], in_=o[:, j, :], func=ACT.Relu)
-            if i == PAIRS - 1:
-                store_token_tile(i, j)
-
-        def store_token_tile(i, j):
-            s, h = divmod(i, ROWS // PAIR)
-            nc.sync.dma_start(
-                out=out[s].rearrange("(p j) f -> p j f", j=ROWS)[:, h * PAIR + j, :], in_=st[i]["o"][:, j, :],
-            )
+            cuts = 2 if i == PAIRS - 1 else 1
+            width = F // cuts
+            for c in range(cuts):
+                f = slice(c * width, (c + 1) * width)
+                if i >= 10 and j == 0:
+                    nc.vector.tensor_scalar(out=o[:, j, f], in0=o[:, j, f], scalar1=0.0, scalar2=None, op0=MAX)
+                else:
+                    nc.scalar.activation(out=o[:, j, f], in_=o[:, j, f], func=ACT.Relu)
+                if i == PAIRS - 1:
+                    s, h = divmod(i, ROWS // PAIR)
+                    nc.sync.dma_start(
+                        out=out[s].rearrange("(p j) f -> p j f", j=ROWS)[:, h * PAIR + j, f], in_=o[:, j, f],
+                    )
 
         def store(i):
             if i == PAIRS - 1:
@@ -319,7 +333,7 @@ def tile_temporalatt_pb_t_w8_kernel(
             )
 
         stages = {
-            "scale": scale, "turn": turn, "gather": gather, "quant1": quant1, "mm1": mm1, "resid": resid,
+            "prep": prepare_weights, "scale": scale, "d": keep_warm, "turn": turn, "gather": gather, "quant1": quant1, "mm1": mm1, "resid": resid,
             "mean": mean, "square": square, "recip": recip, "shift": shift, "norm": norm, "turn2": turn2, "affine": affine, "weave": weave,
             "quant2": quant2,
             "z00": lambda i: half_out(i, 0, 0), "z01": lambda i: half_out(i, 0, 1),
@@ -331,5 +345,3 @@ def tile_temporalatt_pb_t_w8_kernel(
             for name, lag in STEP:
                 if 0 <= k - lag < PAIRS:
                     stages[name](k - lag)
-            if k == 0:
-                prepare_weights()

@@ -27,33 +27,28 @@ PAIR = 2
 PAIRS = SEQS * ROWS // PAIR
 
 STEP = (
-    ("shift", 3),
-    ("d", 5),
-    ("affine", 4),
-    ("scale", 0),
-    ("quant2", 5),
-    ("norm", 3),
-    ("z01", 6),
-    ("z00", 6),
-    ("d", 1),
-    ("mm1", 1),
-    ("weave", 4),
-    ("resid", 1),
-    ("turn", 0),
-    ("prep", 0),
-    ("d", 0),
-    ("square", 2),
-    ("z10", 5),
-    ("z11", 5),
-    ("relu1", 6),
-    ("gather", 0),
-    ("recip", 2),
-    ("store", 7),
-    ("d", 4),
-    ("relu0", 6),
-    ("mean", 1),
-    ("quant1", 0),
-    ("turn2", 3),
+    ("relu0", 54),
+    ("mean", 49),
+    ("turn", 47),
+    ("gather", 47),
+    ("prep", 19),
+    ("z00", 53),
+    ("z01", 53),
+    ("affine", 51),
+    ("mm1", 48),
+    ("square", 49),
+    ("norm", 50),
+    ("resid", 48),
+    ("weave", 51),
+    ("recip", 49),
+    ("scale", 45),
+    ("relu1", 53),
+    ("z10", 52),
+    ("quant1", 47),
+    ("turn2", 50),
+    ("z11", 52),
+    ("shift", 49),
+    ("quant2", 51),
 )
 
 
@@ -64,14 +59,14 @@ def tile_temporalatt_pb_t_w8_kernel(
     nc = tc.nc
     with ExitStack() as ctx:
         keep = ctx.enter_context(tc.tile_pool(name="keep", bufs=1))
-        work = ctx.enter_context(tc.tile_pool(name="work", bufs=3))
+        work = ctx.enter_context(tc.tile_pool(name="work", bufs=4))
         small = ctx.enter_context(tc.tile_pool(name="small", bufs=6))
         psum2 = ctx.enter_context(tc.psum_pool(name="psum2", bufs=2))
         psum1 = ctx.enter_context(tc.psum_pool(name="psum1", bufs=1))
         ctx.enter_context(tc.manual_schedule())
 
-        scale2 = keep.tile([P, PAIR, D], F32, name="scale2")
-        nc.scalar.dma_start(out=scale2[:, 0, :], in_=ax_cat_scale.rearrange("a o k -> (a o k)").partition_broadcast(P))
+        rows = keep.tile([P, PACK], F32, name="rows")
+        nc.scalar.dma_start(out=rows[:], in_=ax_cat_scale.rearrange("a o (p t) -> p (a o t)", t=PACK))
 
         w1s_raw = keep.tile([P, D], U8, name="w1s_raw", align_bytes=64)
         w2s = keep.tile([P, F], U8, name="w2s", align_bytes=64)
@@ -84,40 +79,35 @@ def tile_temporalatt_pb_t_w8_kernel(
             ax[s] = keep.tile([P, ROWS * D], U8, name=f"ax{s}", align_bytes=64)
             nc.sync.dma_start(out=ax[s][:], in_=ax_cat_bytes[s].rearrange("(p j) k -> p (j k)", j=ROWS))
 
-        feat = {}
+        feat = [None] * SEQS
 
-        def load_feat(b, j):
-            feat[b, j] = keep.tile([P, NODES, D], BF16, name=f"feat{b}_{j}")
+        def load_feat(s):
+            b, n = divmod(s, NODES)
+            feat[s] = keep.tile([P, ROWS, D], BF16, name=f"feat{s}")
             nc.sync.dma_start(
-                out=feat[b, j][:],
-                in_=features[b].rearrange("(p j) n d -> p j n d", j=ROWS)[:, j, :, :],
+                out=feat[s][:], in_=features[b].rearrange("(p j) n d -> p n j d", j=ROWS)[:, n, :, :],
             )
 
         load_ax(0)
         w1_raw = keep.tile([P, D], U32, name="w1_raw", align_bytes=64)
+        nc.sync.dma_start(out=w1_raw[:].bitcast(I32), in_=wout_w_words[0].rearrange("p n t -> p (n t)").bitcast(I32))
         for r in range(4):
             nc.sync.dma_start(out=w1s_raw[r:P:32, :].bitcast(I32), in_=wout_w_scales[0][r:16:4, :].bitcast(I32))
-        nc.sync.dma_start(out=w1_raw[:].bitcast(I32), in_=wout_w_words[0].rearrange("p n t -> p (n t)").bitcast(I32))
-        load_feat(0, 0)
-        load_feat(0, 1)
+        load_feat(0)
         gb_bf = keep.tile([P, 2, 16], BF16, name="gb_bf")
         nc.scalar.dma_start(out=gb_bf[:, 0, :PACK], in_=ln_g.rearrange("(p t) -> p t", t=PACK))
         nc.scalar.dma_start(out=gb_bf[:, 1, :PACK], in_=ln_b.rearrange("(p t) -> p t", t=PACK))
-        load_feat(0, 2)
-        load_feat(0, 3)
         load_ax(1)
+        load_feat(1)
         w2 = keep.tile([P, F], U32, name="w2", align_bytes=64)
         nc.sync.dma_start(out=w2[:].bitcast(I32), in_=ff1_w_words[0].rearrange("p n t -> p (n t)").bitcast(I32))
         for r in range(4):
             nc.sync.dma_start(out=w2s[r:P:32, :].bitcast(I32), in_=ff1_w_scales[0][r:16:4, :].bitcast(I32))
         bias = keep.tile([P, F], BF16, name="bias")
         nc.sync.dma_start(out=bias[:], in_=ff1_b.partition_broadcast(P))
-        load_ax(2)
-        load_ax(3)
-        for j in range(ROWS):
-            load_feat(1, j)
-        for s in range(4, SEQS):
+        for s in range(2, SEQS):
             load_ax(s)
+            load_feat(s)
 
         ident = keep.tile([P, P], F32, name="ident")
         make_identity(nc, ident[:])
@@ -127,7 +117,6 @@ def tile_temporalatt_pb_t_w8_kernel(
         nc.vector.tensor_scalar(out=eps[:], in0=zero[:], scalar1=1.0, scalar2=EPS, op0=MULT, op1=ADD)
         warm = keep.tile([P, 1], F32, name="warm")
         nc.scalar.activation(out=warm[:], in_=eps[:], func=ACT.Sqrt)
-        nc.vector.tensor_copy(out=scale2[:, 1, :], in_=scale2[:, 0, :])
         gb = keep.tile([P, 2, PACK], F32, name="gb")
         w1 = keep.tile([P, D], U32, name="w1", align_bytes=64)
         w1s = keep.tile([P, D], U8, name="w1s", align_bytes=64)
@@ -150,39 +139,41 @@ def tile_temporalatt_pb_t_w8_kernel(
         def keep_warm(i):
             nc.tensor.matmul(junk[:], lhsT=ident[:], rhs=ident[:], start=True, stop=True)
 
+        for w in range(8):
+            keep_warm(w)
+
         st = [dict() for unused in range(PAIRS)]
 
         def scale(i):
             s, h = divmod(i, ROWS // PAIR)
-            a = work.tile([P, PAIR, D], BF16, name="a")
-            nc.vector.tensor_tensor(
-                out=a[:].rearrange("p j k -> p (j k)"),
-                in0=ax[s][:, h * PAIR * D:(h + 1) * PAIR * D].bitcast(FP8),
-                in1=scale2[:].rearrange("p j k -> p (j k)"),
-                op=MULT,
-            )
+            a = work.tile([P, PAIR * D], BF16, name="a")
+            nc.scalar.copy(out=a[:], in_=ax[s][:, h * PAIR * D:(h + 1) * PAIR * D].bitcast(FP8))
             st[i]["a"] = a
 
         def turn(i):
             xt = psum1.tile([P, PAIR, 2, P], F32, name="xt")
-            words = st[i]["a"][:].rearrange("p j k -> p (j k)").bitcast(F32)
+            words = st[i]["a"][:].bitcast(F32)
             for j in range(PAIR):
                 for u in range(2):
                     nc.tensor.transpose(xt[:, j, u, :], words[:, j * 256 + u:(j + 1) * 256:2], ident[:])
             st[i]["xt"] = xt
 
         def gather(i):
-            xg = work.tile([P, PAIR * P * PACK], BF16, name="xg", align_bytes=64)
-            nc.scalar.copy(
-                out=xg[:].bitcast(F32).rearrange("p (j r u) -> p j r u", j=PAIR, u=2),
-                in_=st[i]["xt"][:].rearrange("p j u r -> p j r u"),
-            )
+            xg = work.tile([P, PAIR, P * PACK], BF16, name="xg", align_bytes=64)
+            turned = st[i]["xt"][:].bitcast(BF16)
+            factor = rows[:].rearrange("p (o u e) -> p o u e", o=1, u=2).to_broadcast([P, P, 2, 2])
+            for j in range(PAIR):
+                nc.vector.tensor_tensor(
+                    out=xg[:, j, :].rearrange("p (r u e) -> p r u e", u=2, e=2),
+                    in0=turned[:, j, :, :].rearrange("p u (r e) -> p r u e", e=2),
+                    in1=factor, op=MULT,
+                )
             st[i]["xg"] = xg
 
         def quant1(i):
             xq = work.tile([P, PAIR * P], U32, name="xq", align_bytes=64)
             xs = work.tile([P, PAIR * P], U8, name="xs", align_bytes=64)
-            nc.vector.quantize_mx(out=xq[:].bitcast(FP8X4), scales=xs[:], in_=st[i]["xg"][:])
+            nc.vector.quantize_mx(out=xq[:].bitcast(FP8X4), scales=xs[:], in_=st[i]["xg"][:].rearrange("p j w -> p (j w)"))
             st[i]["xq"] = xq, xs
 
         def mm1(i):
@@ -200,7 +191,6 @@ def tile_temporalatt_pb_t_w8_kernel(
 
         def resid(i):
             s, h = divmod(i, ROWS // PAIR)
-            b, n = divmod(s, NODES)
             rs = []
             sums = small.tile([P, PAIR], F32, name="sums")
             for j, y in enumerate(st[i]["y"]):
@@ -208,7 +198,7 @@ def tile_temporalatt_pb_t_w8_kernel(
                 nc.vector.scalar_tensor_tensor(
                     out=r[:].rearrange("p (t m) -> p t m", t=PACK),
                     in0=y[:].rearrange("p (t m) -> p t m", t=PACK), scalar=1.0,
-                    in1=feat[b, h * PAIR + j][:, n, :].rearrange("p (m t) -> p t m", t=PACK),
+                    in1=feat[s][:, h * PAIR + j, :].rearrange("p (m t) -> p t m", t=PACK),
                     op0=MULT, op1=ADD, accum_out=sums[:, j:j + 1],
                 )
                 rs.append(r)
@@ -246,7 +236,7 @@ def tile_temporalatt_pb_t_w8_kernel(
             ns = []
             for j, r in enumerate(st[i]["r"]):
                 nr = work.tile([P, D], F32, name=f"nr{j}")
-                engine = nc.vector if i < 6 else nc.gpsimd
+                engine = nc.vector if False else nc.gpsimd
                 engine.tensor_scalar(
                     out=nr[:], in0=r[:], scalar1=st[i]["rstd"][:, j:j + 1], scalar2=st[i]["nb"][:, j:j + 1],
                     op0=MULT, op1=ADD,
@@ -308,29 +298,19 @@ def tile_temporalatt_pb_t_w8_kernel(
             nc.vector.tensor_tensor(out=st[i]["o"][:, j, f], in0=z[:], in1=bias[:, f], op=ADD)
 
         def relu(i, j):
+            s, h = divmod(i, ROWS // PAIR)
             o = st[i]["o"]
             cuts = 2 if i == PAIRS - 1 else 1
             width = F // cuts
             for c in range(cuts):
                 f = slice(c * width, (c + 1) * width)
-                if i >= 10 and j == 0:
+                if False:
                     nc.vector.tensor_scalar(out=o[:, j, f], in0=o[:, j, f], scalar1=0.0, scalar2=None, op0=MAX)
                 else:
                     nc.scalar.activation(out=o[:, j, f], in_=o[:, j, f], func=ACT.Relu)
-                if i == PAIRS - 1:
-                    s, h = divmod(i, ROWS // PAIR)
-                    nc.sync.dma_start(
-                        out=out[s].rearrange("(p j) f -> p j f", j=ROWS)[:, h * PAIR + j, f], in_=o[:, j, f],
-                    )
-
-        def store(i):
-            if i == PAIRS - 1:
-                return
-            s, h = divmod(i, ROWS // PAIR)
-            nc.sync.dma_start(
-                out=out[s].rearrange("(p j) f -> p j f", j=ROWS)[:, h * PAIR:(h + 1) * PAIR, :],
-                in_=st[i]["o"][:],
-            )
+                nc.sync.dma_start(
+                    out=out[s].rearrange("(p j) f -> p j f", j=ROWS)[:, h * PAIR + j, f], in_=o[:, j, f],
+                )
 
         stages = {
             "prep": prepare_weights, "scale": scale, "d": keep_warm, "turn": turn, "gather": gather, "quant1": quant1, "mm1": mm1, "resid": resid,
@@ -338,7 +318,7 @@ def tile_temporalatt_pb_t_w8_kernel(
             "quant2": quant2,
             "z00": lambda i: half_out(i, 0, 0), "z01": lambda i: half_out(i, 0, 1),
             "z10": lambda i: half_out(i, 1, 0), "z11": lambda i: half_out(i, 1, 1),
-            "relu0": lambda i: relu(i, 0), "relu1": lambda i: relu(i, 1), "store": store,
+            "relu0": lambda i: relu(i, 0), "relu1": lambda i: relu(i, 1),
         }
         deepest = max(lag for name, lag in STEP)
         for k in range(PAIRS + deepest):

@@ -3,10 +3,10 @@ from contextlib import ExitStack
 import concourse.mybir as mybir
 from concourse.masks import make_identity
 
-SEQS, T_LEN, D, F = 8, 512, 512, 1024
+SEQS, TOKENS, D, F = 8, 512, 512, 1024
 NODES = 4
 EPS = 1e-5
-FLOPS = 2 * SEQS * T_LEN * D * (D + F)
+FLOPS = 2 * SEQS * TOKENS * D * (D + F)
 
 F32 = mybir.dt.float32
 BF16 = mybir.dt.bfloat16
@@ -22,34 +22,40 @@ ACT = mybir.ActivationFunctionType
 
 P = 128
 PACK = 4
-ROWS = T_LEN // P
+ROWS = TOKENS // P
 PAIR = 2
-PAIRS = SEQS * ROWS // PAIR
+HALVES = ROWS // PAIR
+PAIRS = SEQS * HALVES
+BANK = 512
 
-STEP = (
-    ("relu0", 54),
-    ("mean", 49),
-    ("turn", 47),
-    ("gather", 47),
-    ("prep", 19),
-    ("z00", 53),
-    ("z01", 53),
-    ("affine", 51),
-    ("mm1", 48),
-    ("square", 49),
-    ("norm", 50),
-    ("resid", 48),
-    ("weave", 51),
-    ("recip", 49),
-    ("scale", 45),
-    ("relu1", 53),
-    ("z10", 52),
-    ("quant1", 47),
-    ("turn2", 50),
-    ("z11", 52),
-    ("shift", 49),
-    ("quant2", 51),
+DELAYS = (
+    ("widen", 0),
+    ("turn", 178),
+    ("scale", 196),
+    ("prepare", 225),
+    ("quantise_ax", 276),
+    ("project", 328),
+    ("residual", 341),
+    ("spread", 460),
+    ("centre", 464),
+    ("busy", 503),
+    ("busy", 535),
+    ("normalise", 548),
+    ("busy", 551),
+    ("turn_back", 583),
+    ("busy", 636),
+    ("affine", 645),
+    ("weave", 680),
+    ("quantise_m", 680),
+    ("expand_11", 744),
+    ("expand_10", 758),
+    ("expand_01", 805),
+    ("expand_00", 827),
+    ("finish_1", 870),
+    ("finish_0", 873),
 )
+
+WARM_UP = 8
 
 
 def tile_temporalatt_pb_t_w8_kernel(
@@ -59,55 +65,66 @@ def tile_temporalatt_pb_t_w8_kernel(
     nc = tc.nc
     with ExitStack() as ctx:
         keep = ctx.enter_context(tc.tile_pool(name="keep", bufs=1))
-        work = ctx.enter_context(tc.tile_pool(name="work", bufs=4))
+        work = ctx.enter_context(tc.tile_pool(name="work", bufs=3))
         small = ctx.enter_context(tc.tile_pool(name="small", bufs=6))
-        psum2 = ctx.enter_context(tc.psum_pool(name="psum2", bufs=2))
         psum1 = ctx.enter_context(tc.psum_pool(name="psum1", bufs=1))
+        psum2 = ctx.enter_context(tc.psum_pool(name="psum2", bufs=2))
         ctx.enter_context(tc.manual_schedule())
 
-        rows = keep.tile([P, PACK], F32, name="rows")
-        nc.scalar.dma_start(out=rows[:], in_=ax_cat_scale.rearrange("a o (p t) -> p (a o t)", t=PACK))
+        factors = keep.tile([P, PACK], F32, name="factors")
+        nc.scalar.dma_start(out=factors[:], in_=ax_cat_scale.rearrange("a o (p t) -> p (a o t)", t=PACK))
 
-        w1s_raw = keep.tile([P, D], U8, name="w1s_raw", align_bytes=64)
-        w2s = keep.tile([P, F], U8, name="w2s", align_bytes=64)
-        nc.vector.memset(w1s_raw[:].bitcast(I32), 0)
-        nc.vector.memset(w2s[:].bitcast(I32), 0)
+        w1_scales_raw = keep.tile([P, D], U8, name="w1_scales_raw", align_bytes=64)
+        w2_scales = keep.tile([P, F], U8, name="w2_scales", align_bytes=64)
+        nc.vector.memset(w1_scales_raw[:].bitcast(I32), 0)
+        nc.vector.memset(w2_scales[:].bitcast(I32), 0)
 
-        ax = [None] * SEQS
+        def load_scale_rows(tile, scales):
+            for r in range(4):
+                nc.sync.dma_start(out=tile[r:P:32, :].bitcast(I32), in_=scales[0][r:16:4, :].bitcast(I32))
 
-        def load_ax(s):
-            ax[s] = keep.tile([P, ROWS * D], U8, name=f"ax{s}", align_bytes=64)
-            nc.sync.dma_start(out=ax[s][:], in_=ax_cat_bytes[s].rearrange("(p j) k -> p (j k)", j=ROWS))
+        def load_words(tile, words):
+            nc.sync.dma_start(out=tile[:].bitcast(I32), in_=words[0].rearrange("p n t -> p (n t)").bitcast(I32))
 
+        codes_in = [None] * SEQS
         feat = [None] * SEQS
 
-        def load_feat(s):
+        def load_codes(s, pieces=1):
+            codes_in[s] = keep.tile([P, ROWS * D], U8, name=f"codes_in{s}", align_bytes=64)
+            rows = ax_cat_bytes[s].rearrange("(p j) k -> p (j k)", j=ROWS)
+            width = ROWS * D // pieces
+            for c in range(pieces):
+                cols = slice(c * width, (c + 1) * width)
+                nc.sync.dma_start(out=codes_in[s][:, cols], in_=rows[:, cols])
+
+        def load_features(s):
             b, n = divmod(s, NODES)
             feat[s] = keep.tile([P, ROWS, D], BF16, name=f"feat{s}")
-            nc.sync.dma_start(
-                out=feat[s][:], in_=features[b].rearrange("(p j) n d -> p n j d", j=ROWS)[:, n, :, :],
-            )
+            nc.sync.dma_start(out=feat[s][:], in_=features[b].rearrange("(p j) n d -> p n j d", j=ROWS)[:, n, :, :])
 
-        load_ax(0)
         w1_raw = keep.tile([P, D], U32, name="w1_raw", align_bytes=64)
-        nc.sync.dma_start(out=w1_raw[:].bitcast(I32), in_=wout_w_words[0].rearrange("p n t -> p (n t)").bitcast(I32))
-        for r in range(4):
-            nc.sync.dma_start(out=w1s_raw[r:P:32, :].bitcast(I32), in_=wout_w_scales[0][r:16:4, :].bitcast(I32))
-        load_feat(0)
-        gb_bf = keep.tile([P, 2, 16], BF16, name="gb_bf")
-        nc.scalar.dma_start(out=gb_bf[:, 0, :PACK], in_=ln_g.rearrange("(p t) -> p t", t=PACK))
-        nc.scalar.dma_start(out=gb_bf[:, 1, :PACK], in_=ln_b.rearrange("(p t) -> p t", t=PACK))
-        load_ax(1)
-        load_feat(1)
         w2 = keep.tile([P, F], U32, name="w2", align_bytes=64)
-        nc.sync.dma_start(out=w2[:].bitcast(I32), in_=ff1_w_words[0].rearrange("p n t -> p (n t)").bitcast(I32))
-        for r in range(4):
-            nc.sync.dma_start(out=w2s[r:P:32, :].bitcast(I32), in_=ff1_w_scales[0][r:16:4, :].bitcast(I32))
         bias = keep.tile([P, F], BF16, name="bias")
+        norm_raw = keep.tile([P, 2, 16], BF16, name="norm_raw")
+
+        load_codes(0, pieces=HALVES)
+        load_words(w1_raw, wout_w_words)
+        load_scale_rows(w1_scales_raw, wout_w_scales)
+        load_features(0)
+        nc.scalar.dma_start(out=norm_raw[:, 0, :PACK], in_=ln_g.rearrange("(p t) -> p t", t=PACK))
+        nc.scalar.dma_start(out=norm_raw[:, 1, :PACK], in_=ln_b.rearrange("(p t) -> p t", t=PACK))
+        load_codes(1)
+        load_codes(2)
+        load_features(1)
+        load_codes(3)
+        load_words(w2, ff1_w_words)
+        load_scale_rows(w2_scales, ff1_w_scales)
+        load_features(2)
         nc.sync.dma_start(out=bias[:], in_=ff1_b.partition_broadcast(P))
-        for s in range(2, SEQS):
-            load_ax(s)
-            load_feat(s)
+        load_features(3)
+        for s in range(4, SEQS):
+            load_codes(s)
+            load_features(s)
 
         ident = keep.tile([P, P], F32, name="ident")
         make_identity(nc, ident[:])
@@ -115,13 +132,14 @@ def tile_temporalatt_pb_t_w8_kernel(
         nc.vector.memset(zero[:], 0.0)
         eps = keep.tile([P, 1], F32, name="eps")
         nc.vector.tensor_scalar(out=eps[:], in0=zero[:], scalar1=1.0, scalar2=EPS, op0=MULT, op1=ADD)
-        warm = keep.tile([P, 1], F32, name="warm")
-        nc.scalar.activation(out=warm[:], in_=eps[:], func=ACT.Sqrt)
-        gb = keep.tile([P, 2, PACK], F32, name="gb")
-        w1 = keep.tile([P, D], U32, name="w1", align_bytes=64)
-        w1s = keep.tile([P, D], U8, name="w1s", align_bytes=64)
+        first = keep.tile([P, 1], F32, name="first")
+        nc.scalar.activation(out=first[:], in_=eps[:], func=ACT.Abs_reciprocal_sqrt)
 
-        def prepare_weights(i):
+        gain_shift = keep.tile([P, 2, PACK], F32, name="gain_shift")
+        w1 = keep.tile([P, D], U32, name="w1", align_bytes=64)
+        w1_scales = keep.tile([P, D], U8, name="w1_scales", align_bytes=64)
+
+        def prepare(i):
             if i > 0:
                 return
             nc.vector.tensor_copy(
@@ -129,199 +147,179 @@ def tile_temporalatt_pb_t_w8_kernel(
                 in_=w1_raw[:].bitcast(I32).rearrange("p (m t) -> p t m", t=PACK),
             )
             nc.vector.tensor_copy(
-                out=w1s[:].rearrange("p (t m) -> p t m", t=PACK),
-                in_=w1s_raw[:].rearrange("p (m t) -> p t m", t=PACK),
+                out=w1_scales[:].rearrange("p (t m) -> p t m", t=PACK),
+                in_=w1_scales_raw[:].rearrange("p (m t) -> p t m", t=PACK),
             )
-            nc.vector.tensor_copy(out=gb[:], in_=gb_bf[:, :, :PACK])
+            nc.vector.tensor_copy(out=gain_shift[:], in_=norm_raw[:, :, :PACK])
 
         junk = psum1.tile([P, P], F32, name="junk")
 
-        def keep_warm(i):
+        def busy(i):
             nc.tensor.matmul(junk[:], lhsT=ident[:], rhs=ident[:], start=True, stop=True)
 
-        for w in range(8):
-            keep_warm(w)
+        for w in range(WARM_UP):
+            busy(0)
 
-        st = [dict() for unused in range(PAIRS)]
+        live = [dict() for i in range(PAIRS)]
 
-        def scale(i):
-            s, h = divmod(i, ROWS // PAIR)
-            a = work.tile([P, PAIR * D], BF16, name="a")
-            nc.scalar.copy(out=a[:], in_=ax[s][:, h * PAIR * D:(h + 1) * PAIR * D].bitcast(FP8))
-            st[i]["a"] = a
+        def widen(i):
+            s, h = divmod(i, HALVES)
+            wide = work.tile([P, PAIR * D], BF16, name="wide")
+            nc.scalar.copy(out=wide[:], in_=codes_in[s][:, h * PAIR * D:(h + 1) * PAIR * D].bitcast(FP8))
+            live[i]["wide"] = wide
 
         def turn(i):
-            xt = psum1.tile([P, PAIR, 2, P], F32, name="xt")
-            words = st[i]["a"][:].bitcast(F32)
+            turned = psum1.tile([P, PAIR, 2, P], F32, name="turned")
+            words = live[i]["wide"][:].bitcast(F32)
             for j in range(PAIR):
                 for u in range(2):
-                    nc.tensor.transpose(xt[:, j, u, :], words[:, j * 256 + u:(j + 1) * 256:2], ident[:])
-            st[i]["xt"] = xt
+                    nc.tensor.transpose(turned[:, j, u, :], words[:, j * D // 2 + u:(j + 1) * D // 2:2], ident[:])
+            live[i]["turned"] = turned
 
-        def gather(i):
-            xg = work.tile([P, PAIR, P * PACK], BF16, name="xg", align_bytes=64)
-            turned = st[i]["xt"][:].bitcast(BF16)
-            factor = rows[:].rearrange("p (o u e) -> p o u e", o=1, u=2).to_broadcast([P, P, 2, 2])
+        def scale(i):
+            scaled = work.tile([P, PAIR, P * PACK], BF16, name="scaled", align_bytes=64)
+            halves = live[i]["turned"][:].bitcast(BF16)
+            factor = factors[:].rearrange("p (o u e) -> p o u e", o=1, u=2).to_broadcast([P, P, 2, 2])
             for j in range(PAIR):
                 nc.vector.tensor_tensor(
-                    out=xg[:, j, :].rearrange("p (r u e) -> p r u e", u=2, e=2),
-                    in0=turned[:, j, :, :].rearrange("p u (r e) -> p r u e", e=2),
+                    out=scaled[:, j, :].rearrange("p (r u e) -> p r u e", u=2, e=2),
+                    in0=halves[:, j, :, :].rearrange("p u (r e) -> p r u e", e=2),
                     in1=factor, op=MULT,
                 )
-            st[i]["xg"] = xg
+            live[i]["scaled"] = scaled
 
-        def quant1(i):
-            xq = work.tile([P, PAIR * P], U32, name="xq", align_bytes=64)
-            xs = work.tile([P, PAIR * P], U8, name="xs", align_bytes=64)
-            nc.vector.quantize_mx(out=xq[:].bitcast(FP8X4), scales=xs[:], in_=st[i]["xg"][:].rearrange("p j w -> p (j w)"))
-            st[i]["xq"] = xq, xs
+        def quantise_ax(i):
+            codes = work.tile([P, PAIR * P], U32, name="ax_codes", align_bytes=64)
+            scales = work.tile([P, PAIR * P], U8, name="ax_scales", align_bytes=64)
+            nc.vector.quantize_mx(
+                out=codes[:].bitcast(FP8X4), scales=scales[:], in_=live[i]["scaled"][:].rearrange("p j w -> p (j w)"),
+            )
+            live[i]["ax"] = codes, scales
 
-        def mm1(i):
-            xq, xs = st[i]["xq"]
-            ys = []
+        def project(i):
+            codes, scales = live[i]["ax"]
+            live[i]["y"] = []
             for j in range(PAIR):
-                c = slice(j * P, (j + 1) * P)
+                cols = slice(j * P, (j + 1) * P)
                 y = psum2.tile([P, D], F32, name="y")
                 nc.tensor.matmul_mx(
-                    out=y[:], lhsT=xq[:, c].bitcast(FP8X4), lhsT_scale=xs[:, c],
-                    rhs=w1[:].bitcast(FP8X4), rhs_scale=w1s[:], start=True, stop=True,
+                    out=y[:], lhsT=codes[:, cols].bitcast(FP8X4), lhsT_scale=scales[:, cols],
+                    rhs=w1[:].bitcast(FP8X4), rhs_scale=w1_scales[:], start=True, stop=True,
                 )
-                ys.append(y)
-            st[i]["y"] = ys
+                live[i]["y"].append(y)
 
-        def resid(i):
-            s, h = divmod(i, ROWS // PAIR)
-            rs = []
+        def residual(i):
+            s, h = divmod(i, HALVES)
             sums = small.tile([P, PAIR], F32, name="sums")
-            for j, y in enumerate(st[i]["y"]):
+            live[i]["r"] = []
+            for j in range(PAIR):
                 r = work.tile([P, D], F32, name=f"r{j}")
                 nc.vector.scalar_tensor_tensor(
                     out=r[:].rearrange("p (t m) -> p t m", t=PACK),
-                    in0=y[:].rearrange("p (t m) -> p t m", t=PACK), scalar=1.0,
+                    in0=live[i]["y"][j][:].rearrange("p (t m) -> p t m", t=PACK), scalar=1.0,
                     in1=feat[s][:, h * PAIR + j, :].rearrange("p (m t) -> p t m", t=PACK),
                     op0=MULT, op1=ADD, accum_out=sums[:, j:j + 1],
                 )
-                rs.append(r)
-            st[i]["r"] = rs
-            st[i]["sums"] = sums
+                live[i]["r"].append(r)
+            live[i]["sums"] = sums
 
-        def mean(i):
-            nm = small.tile([P, PAIR], F32, name="nm")
-            nc.scalar.activation(out=nm[:], in_=st[i]["sums"][:], func=ACT.Copy, scale=-1.0 / D)
-            st[i]["nm"] = nm
-
-        def square(i):
-            ssq = small.tile([P, PAIR], F32, name="ssq")
+        def spread(i):
+            squares = small.tile([P, PAIR], F32, name="squares")
             for j in range(PAIR):
-                sq = work.tile([P, D], BF16, name="sq")
+                unread = work.tile([P, D], BF16, name="unread")
                 nc.scalar.activation(
-                    out=sq[:], in_=st[i]["r"][j][:], func=ACT.Square,
-                    bias=st[i]["nm"][:, j:j + 1], accum_out=ssq[:, j:j + 1],
+                    out=unread[:], in_=live[i]["r"][j][:], func=ACT.Square,
+                    scale=-float(D), bias=live[i]["sums"][:, j:j + 1], accum_out=squares[:, j:j + 1],
                 )
-            std = small.tile([P, PAIR], F32, name="std")
-            nc.scalar.activation(out=std[:], in_=ssq[:], func=ACT.Sqrt, scale=1.0 / D, bias=eps[:])
-            st[i]["std"] = std
-
-        def recip(i):
             rstd = small.tile([P, PAIR], F32, name="rstd")
-            nc.vector.reciprocal(out=rstd[:], in_=st[i]["std"][:])
-            st[i]["rstd"] = rstd
+            nc.scalar.activation(out=rstd[:], in_=squares[:], func=ACT.Abs_reciprocal_sqrt, scale=1.0 / D**3, bias=eps[:])
+            live[i]["rstd"] = rstd
 
-        def shift(i):
-            nb = small.tile([P, PAIR], F32, name="nb")
-            nc.vector.tensor_tensor(out=nb[:], in0=st[i]["nm"][:], in1=st[i]["rstd"][:], op=MULT)
-            st[i]["nb"] = nb
+        def centre(i):
+            offset = small.tile([P, PAIR], F32, name="offset")
+            nc.vector.scalar_tensor_tensor(
+                out=offset[:], in0=live[i]["sums"][:], scalar=-1.0 / D, in1=live[i]["rstd"][:], op0=MULT, op1=MULT,
+            )
+            live[i]["offset"] = offset
 
-        def norm(i):
-            ns = []
-            for j, r in enumerate(st[i]["r"]):
-                nr = work.tile([P, D], F32, name=f"nr{j}")
-                engine = nc.vector if False else nc.gpsimd
-                engine.tensor_scalar(
-                    out=nr[:], in0=r[:], scalar1=st[i]["rstd"][:, j:j + 1], scalar2=st[i]["nb"][:, j:j + 1],
-                    op0=MULT, op1=ADD,
+        def normalise(i):
+            live[i]["normed"] = []
+            for j in range(PAIR):
+                normed = work.tile([P, D], F32, name=f"normed{j}")
+                nc.gpsimd.tensor_scalar(
+                    out=normed[:], in0=live[i]["r"][j][:], scalar1=live[i]["rstd"][:, j:j + 1],
+                    scalar2=live[i]["offset"][:, j:j + 1], op0=MULT, op1=ADD,
                 )
-                ns.append(nr)
-            st[i]["n"] = ns
+                live[i]["normed"].append(normed)
 
-        def turn2(i):
-            ns = st[i]["n"]
-            nts = []
+        def turn_back(i):
+            live[i]["channels"] = []
             for u in range(2):
-                nt = psum1.tile([P, 2, PAIR, P], F32, name=f"nt{u}")
+                channels = psum1.tile([P, 2, PAIR, P], F32, name=f"channels{u}")
                 for e in range(2):
                     t = 2 * u + e
                     for j in range(PAIR):
-                        nc.tensor.transpose(nt[:, e, j, :], ns[j][:, t * P:(t + 1) * P], ident[:])
-                nts.append(nt)
-            st[i]["nt"] = nts
+                        nc.tensor.transpose(channels[:, e, j, :], live[i]["normed"][j][:, t * P:(t + 1) * P], ident[:])
+                live[i]["channels"].append(channels)
 
         def affine(i):
             planes = work.tile([P, PACK, PAIR * P], BF16, name="planes")
-            for u, nt in enumerate(st[i]["nt"]):
-                for e in range(2):
-                    t = 2 * u + e
-                    nc.scalar.activation(
-                        out=planes[:, t, :], in_=nt[:, e, :, :].rearrange("p j r -> p (j r)"), func=ACT.Identity,
-                        scale=gb[:, 0, t:t + 1], bias=gb[:, 1, t:t + 1],
-                    )
-            st[i]["planes"] = planes
+            for t in range(PACK):
+                nc.scalar.activation(
+                    out=planes[:, t, :], in_=live[i]["channels"][t // 2][:, t % 2, :, :].rearrange("p j r -> p (j r)"),
+                    func=ACT.Identity, scale=gain_shift[:, 0, t:t + 1], bias=gain_shift[:, 1, t:t + 1],
+                )
+            live[i]["planes"] = planes
 
         def weave(i):
-            mg = work.tile([P, PAIR * P * PACK], BF16, name="mg", align_bytes=64)
-            woven = mg[:].rearrange("p (r t) -> p r t", t=PACK)
-            planes = st[i]["planes"][:].rearrange("p t r -> p r t")
-            if False:
-                nc.scalar.copy(out=woven, in_=planes)
-            elif True:
-                nc.gpsimd.tensor_scalar(out=woven, in0=planes, scalar1=1.0, scalar2=0.0, op0=MULT, op1=ADD)
-            else:
-                nc.vector.tensor_copy(out=woven, in_=planes)
-            st[i]["mg"] = mg
-
-        def quant2(i):
-            mq = work.tile([P, PAIR * P], U32, name="mq", align_bytes=64)
-            ms = work.tile([P, PAIR * P], U8, name="ms", align_bytes=64)
-            nc.vector.quantize_mx(out=mq[:].bitcast(FP8X4), scales=ms[:], in_=st[i]["mg"][:])
-            st[i]["mq"] = mq, ms
-            st[i]["o"] = work.tile([P, PAIR, F], F32, name="o")
-
-        def half_out(i, j, h):
-            mq, ms = st[i]["mq"]
-            c = slice(j * P, (j + 1) * P)
-            f = slice(h * 512, (h + 1) * 512)
-            z = psum2.tile([P, 512], F32, name="z")
-            nc.tensor.matmul_mx(
-                out=z[:], lhsT=mq[:, c].bitcast(FP8X4), lhsT_scale=ms[:, c],
-                rhs=w2[:, f].bitcast(FP8X4), rhs_scale=w2s[:, f], start=True, stop=True,
+            woven = work.tile([P, PAIR * P * PACK], BF16, name="woven", align_bytes=64)
+            nc.gpsimd.tensor_scalar(
+                out=woven[:].rearrange("p (r t) -> p r t", t=PACK), in0=live[i]["planes"][:].rearrange("p t r -> p r t"),
+                scalar1=1.0, scalar2=0.0, op0=MULT, op1=ADD,
             )
-            nc.vector.tensor_tensor(out=st[i]["o"][:, j, f], in0=z[:], in1=bias[:, f], op=ADD)
+            live[i]["woven"] = woven
 
-        def relu(i, j):
-            s, h = divmod(i, ROWS // PAIR)
-            o = st[i]["o"]
-            cuts = 2 if i == PAIRS - 1 else 1
-            width = F // cuts
-            for c in range(cuts):
-                f = slice(c * width, (c + 1) * width)
-                if False:
-                    nc.vector.tensor_scalar(out=o[:, j, f], in0=o[:, j, f], scalar1=0.0, scalar2=None, op0=MAX)
+        def quantise_m(i):
+            codes = work.tile([P, PAIR * P], U32, name="m_codes", align_bytes=64)
+            scales = work.tile([P, PAIR * P], U8, name="m_scales", align_bytes=64)
+            nc.vector.quantize_mx(out=codes[:].bitcast(FP8X4), scales=scales[:], in_=live[i]["woven"][:])
+            live[i]["m"] = codes, scales
+            live[i]["result"] = work.tile([P, PAIR, F], F32, name="result")
+
+        def expand(i, j, h):
+            codes, scales = live[i]["m"]
+            tokens = slice(j * P, (j + 1) * P)
+            cols = slice(h * BANK, (h + 1) * BANK)
+            z = psum2.tile([P, BANK], F32, name="z")
+            nc.tensor.matmul_mx(
+                out=z[:], lhsT=codes[:, tokens].bitcast(FP8X4), lhsT_scale=scales[:, tokens],
+                rhs=w2[:, cols].bitcast(FP8X4), rhs_scale=w2_scales[:, cols], start=True, stop=True,
+            )
+            nc.vector.tensor_tensor(out=live[i]["result"][:, j, cols], in0=z[:], in1=bias[:, cols], op=ADD)
+
+        def finish(i, j):
+            s, h = divmod(i, HALVES)
+            result = live[i]["result"]
+            pieces = 2 if i == PAIRS - 1 else 1
+            width = F // pieces
+            for c in range(pieces):
+                cols = slice(c * width, (c + 1) * width)
+                if i % 4 == 3 and j == 0:
+                    nc.vector.tensor_scalar(out=result[:, j, cols], in0=result[:, j, cols], scalar1=0.0, scalar2=None, op0=MAX)
                 else:
-                    nc.scalar.activation(out=o[:, j, f], in_=o[:, j, f], func=ACT.Relu)
+                    nc.scalar.activation(out=result[:, j, cols], in_=result[:, j, cols], func=ACT.Relu)
                 nc.sync.dma_start(
-                    out=out[s].rearrange("(p j) f -> p j f", j=ROWS)[:, h * PAIR + j, f], in_=o[:, j, f],
+                    out=out[s].rearrange("(p j) f -> p j f", j=ROWS)[:, h * PAIR + j, cols], in_=result[:, j, cols],
                 )
 
         stages = {
-            "prep": prepare_weights, "scale": scale, "d": keep_warm, "turn": turn, "gather": gather, "quant1": quant1, "mm1": mm1, "resid": resid,
-            "mean": mean, "square": square, "recip": recip, "shift": shift, "norm": norm, "turn2": turn2, "affine": affine, "weave": weave,
-            "quant2": quant2,
-            "z00": lambda i: half_out(i, 0, 0), "z01": lambda i: half_out(i, 0, 1),
-            "z10": lambda i: half_out(i, 1, 0), "z11": lambda i: half_out(i, 1, 1),
-            "relu0": lambda i: relu(i, 0), "relu1": lambda i: relu(i, 1),
+            "prepare": prepare, "widen": widen, "turn": turn, "scale": scale, "quantise_ax": quantise_ax,
+            "project": project, "residual": residual, "spread": spread, "centre": centre, "normalise": normalise,
+            "turn_back": turn_back, "affine": affine, "weave": weave, "quantise_m": quantise_m, "busy": busy,
+            "expand_00": lambda i: expand(i, 0, 0), "expand_01": lambda i: expand(i, 0, 1),
+            "expand_10": lambda i: expand(i, 1, 0), "expand_11": lambda i: expand(i, 1, 1),
+            "finish_0": lambda i: finish(i, 0), "finish_1": lambda i: finish(i, 1),
         }
-        deepest = max(lag for name, lag in STEP)
-        for k in range(PAIRS + deepest):
-            for name, lag in STEP:
-                if 0 <= k - lag < PAIRS:
-                    stages[name](k - lag)
+        text = [(100 * i + delay, place, i) for i in range(PAIRS) for place, (name, delay) in enumerate(DELAYS)]
+        for when, place, i in sorted(text):
+            stages[DELAYS[place][0]](i)

from contextlib import ExitStack

import concourse.mybir as mybir
from concourse.masks import make_identity

SEQS, TOKENS, D, F = 8, 512, 512, 1024
NODES = 4
EPS = 1e-5
FLOPS = 2 * SEQS * TOKENS * D * (D + F)

F32 = mybir.dt.float32
BF16 = mybir.dt.bfloat16
U32 = mybir.dt.uint32
I32 = mybir.dt.int32
U8 = mybir.dt.uint8
FP8 = mybir.dt.float8_e4m3fn
FP8X4 = mybir.dt.float8_e4m3fn_x4
ADD = mybir.AluOpType.add
MULT = mybir.AluOpType.mult
MAX = mybir.AluOpType.max
ACT = mybir.ActivationFunctionType

P = 128
PACK = 4
ROWS = TOKENS // P
PAIR = 2
HALVES = ROWS // PAIR
PAIRS = SEQS * HALVES
BANK = 512

DELAYS = (
    ("widen", 0),
    ("turn", 178),
    ("scale", 196),
    ("prepare", 225),
    ("quantise_ax", 276),
    ("project", 328),
    ("residual", 341),
    ("spread", 460),
    ("centre", 464),
    ("busy", 503),
    ("busy", 535),
    ("normalise", 548),
    ("busy", 551),
    ("turn_back", 583),
    ("busy", 636),
    ("affine", 645),
    ("weave", 680),
    ("quantise_m", 680),
    ("expand_11", 744),
    ("expand_10", 758),
    ("expand_01", 805),
    ("expand_00", 827),
    ("finish_1", 870),
    ("finish_0", 873),
)

WARM_UP = 8


def tile_temporalatt_pb_t_w8_kernel(
    tc, ax_cat_bytes, ax_cat_scale, features, wout_w_words, wout_w_scales,
    ln_g, ln_b, ff1_w_words, ff1_w_scales, ff1_b, out,
):
    nc = tc.nc
    with ExitStack() as ctx:
        keep = ctx.enter_context(tc.tile_pool(name="keep", bufs=1))
        work = ctx.enter_context(tc.tile_pool(name="work", bufs=3))
        small = ctx.enter_context(tc.tile_pool(name="small", bufs=6))
        psum1 = ctx.enter_context(tc.psum_pool(name="psum1", bufs=1))
        psum2 = ctx.enter_context(tc.psum_pool(name="psum2", bufs=2))
        ctx.enter_context(tc.manual_schedule())

        factors = keep.tile([P, PACK], F32, name="factors")
        nc.scalar.dma_start(out=factors[:], in_=ax_cat_scale.rearrange("a o (p t) -> p (a o t)", t=PACK))

        w1_scales_raw = keep.tile([P, D], U8, name="w1_scales_raw", align_bytes=64)
        w2_scales = keep.tile([P, F], U8, name="w2_scales", align_bytes=64)
        nc.vector.memset(w1_scales_raw[:].bitcast(I32), 0)
        nc.vector.memset(w2_scales[:].bitcast(I32), 0)

        def load_scale_rows(tile, scales):
            for r in range(4):
                nc.sync.dma_start(out=tile[r:P:32, :].bitcast(I32), in_=scales[0][r:16:4, :].bitcast(I32))

        def load_words(tile, words):
            nc.sync.dma_start(out=tile[:].bitcast(I32), in_=words[0].rearrange("p n t -> p (n t)").bitcast(I32))

        codes_in = [None] * SEQS
        feat = [None] * SEQS

        def load_codes(s, pieces=1):
            codes_in[s] = keep.tile([P, ROWS * D], U8, name=f"codes_in{s}", align_bytes=64)
            rows = ax_cat_bytes[s].rearrange("(p j) k -> p (j k)", j=ROWS)
            width = ROWS * D // pieces
            for c in range(pieces):
                cols = slice(c * width, (c + 1) * width)
                nc.sync.dma_start(out=codes_in[s][:, cols], in_=rows[:, cols])

        def load_features(s):
            b, n = divmod(s, NODES)
            feat[s] = keep.tile([P, ROWS, D], BF16, name=f"feat{s}")
            nc.sync.dma_start(out=feat[s][:], in_=features[b].rearrange("(p j) n d -> p n j d", j=ROWS)[:, n, :, :])

        w1_raw = keep.tile([P, D], U32, name="w1_raw", align_bytes=64)
        w2 = keep.tile([P, F], U32, name="w2", align_bytes=64)
        bias = keep.tile([P, F], BF16, name="bias")
        norm_raw = keep.tile([P, 2, 16], BF16, name="norm_raw")

        load_codes(0, pieces=HALVES)
        load_words(w1_raw, wout_w_words)
        load_scale_rows(w1_scales_raw, wout_w_scales)
        load_features(0)
        nc.scalar.dma_start(out=norm_raw[:, 0, :PACK], in_=ln_g.rearrange("(p t) -> p t", t=PACK))
        nc.scalar.dma_start(out=norm_raw[:, 1, :PACK], in_=ln_b.rearrange("(p t) -> p t", t=PACK))
        load_codes(1)
        load_codes(2)
        load_features(1)
        load_codes(3)
        load_words(w2, ff1_w_words)
        load_scale_rows(w2_scales, ff1_w_scales)
        load_features(2)
        nc.sync.dma_start(out=bias[:], in_=ff1_b.partition_broadcast(P))
        load_features(3)
        for s in range(4, SEQS):
            load_codes(s)
            load_features(s)

        ident = keep.tile([P, P], F32, name="ident")
        make_identity(nc, ident[:])
        zero = keep.tile([P, 1], F32, name="zero")
        nc.vector.memset(zero[:], 0.0)
        eps = keep.tile([P, 1], F32, name="eps")
        nc.vector.tensor_scalar(out=eps[:], in0=zero[:], scalar1=1.0, scalar2=EPS, op0=MULT, op1=ADD)
        first = keep.tile([P, 1], F32, name="first")
        nc.scalar.activation(out=first[:], in_=eps[:], func=ACT.Abs_reciprocal_sqrt)

        gain_shift = keep.tile([P, 2, PACK], F32, name="gain_shift")
        w1 = keep.tile([P, D], U32, name="w1", align_bytes=64)
        w1_scales = keep.tile([P, D], U8, name="w1_scales", align_bytes=64)

        def prepare(i):
            if i > 0:
                return
            nc.vector.tensor_copy(
                out=w1[:].bitcast(I32).rearrange("p (t m) -> p t m", t=PACK),
                in_=w1_raw[:].bitcast(I32).rearrange("p (m t) -> p t m", t=PACK),
            )
            nc.vector.tensor_copy(
                out=w1_scales[:].rearrange("p (t m) -> p t m", t=PACK),
                in_=w1_scales_raw[:].rearrange("p (m t) -> p t m", t=PACK),
            )
            nc.vector.tensor_copy(out=gain_shift[:], in_=norm_raw[:, :, :PACK])

        junk = psum1.tile([P, P], F32, name="junk")

        def busy(i):
            nc.tensor.matmul(junk[:], lhsT=ident[:], rhs=ident[:], start=True, stop=True)

        for w in range(WARM_UP):
            busy(0)

        live = [dict() for i in range(PAIRS)]

        def widen(i):
            s, h = divmod(i, HALVES)
            wide = work.tile([P, PAIR * D], BF16, name="wide")
            nc.scalar.copy(out=wide[:], in_=codes_in[s][:, h * PAIR * D:(h + 1) * PAIR * D].bitcast(FP8))
            live[i]["wide"] = wide

        def turn(i):
            turned = psum1.tile([P, PAIR, 2, P], F32, name="turned")
            words = live[i]["wide"][:].bitcast(F32)
            for j in range(PAIR):
                for u in range(2):
                    nc.tensor.transpose(turned[:, j, u, :], words[:, j * D // 2 + u:(j + 1) * D // 2:2], ident[:])
            live[i]["turned"] = turned

        def scale(i):
            scaled = work.tile([P, PAIR, P * PACK], BF16, name="scaled", align_bytes=64)
            halves = live[i]["turned"][:].bitcast(BF16)
            factor = factors[:].rearrange("p (o u e) -> p o u e", o=1, u=2).to_broadcast([P, P, 2, 2])
            for j in range(PAIR):
                nc.vector.tensor_tensor(
                    out=scaled[:, j, :].rearrange("p (r u e) -> p r u e", u=2, e=2),
                    in0=halves[:, j, :, :].rearrange("p u (r e) -> p r u e", e=2),
                    in1=factor, op=MULT,
                )
            live[i]["scaled"] = scaled

        def quantise_ax(i):
            codes = work.tile([P, PAIR * P], U32, name="ax_codes", align_bytes=64)
            scales = work.tile([P, PAIR * P], U8, name="ax_scales", align_bytes=64)
            nc.vector.quantize_mx(
                out=codes[:].bitcast(FP8X4), scales=scales[:], in_=live[i]["scaled"][:].rearrange("p j w -> p (j w)"),
            )
            live[i]["ax"] = codes, scales

        def project(i):
            codes, scales = live[i]["ax"]
            live[i]["y"] = []
            for j in range(PAIR):
                cols = slice(j * P, (j + 1) * P)
                y = psum2.tile([P, D], F32, name="y")
                nc.tensor.matmul_mx(
                    out=y[:], lhsT=codes[:, cols].bitcast(FP8X4), lhsT_scale=scales[:, cols],
                    rhs=w1[:].bitcast(FP8X4), rhs_scale=w1_scales[:], start=True, stop=True,
                )
                live[i]["y"].append(y)

        def residual(i):
            s, h = divmod(i, HALVES)
            sums = small.tile([P, PAIR], F32, name="sums")
            live[i]["r"] = []
            for j in range(PAIR):
                r = work.tile([P, D], F32, name=f"r{j}")
                nc.vector.scalar_tensor_tensor(
                    out=r[:].rearrange("p (t m) -> p t m", t=PACK),
                    in0=live[i]["y"][j][:].rearrange("p (t m) -> p t m", t=PACK), scalar=1.0,
                    in1=feat[s][:, h * PAIR + j, :].rearrange("p (m t) -> p t m", t=PACK),
                    op0=MULT, op1=ADD, accum_out=sums[:, j:j + 1],
                )
                live[i]["r"].append(r)
            live[i]["sums"] = sums

        def spread(i):
            squares = small.tile([P, PAIR], F32, name="squares")
            for j in range(PAIR):
                unread = work.tile([P, D], BF16, name="unread")
                nc.scalar.activation(
                    out=unread[:], in_=live[i]["r"][j][:], func=ACT.Square,
                    scale=-float(D), bias=live[i]["sums"][:, j:j + 1], accum_out=squares[:, j:j + 1],
                )
            rstd = small.tile([P, PAIR], F32, name="rstd")
            nc.scalar.activation(out=rstd[:], in_=squares[:], func=ACT.Abs_reciprocal_sqrt, scale=1.0 / D**3, bias=eps[:])
            live[i]["rstd"] = rstd

        def centre(i):
            offset = small.tile([P, PAIR], F32, name="offset")
            nc.vector.scalar_tensor_tensor(
                out=offset[:], in0=live[i]["sums"][:], scalar=-1.0 / D, in1=live[i]["rstd"][:], op0=MULT, op1=MULT,
            )
            live[i]["offset"] = offset

        def normalise(i):
            live[i]["normed"] = []
            for j in range(PAIR):
                normed = work.tile([P, D], F32, name=f"normed{j}")
                nc.gpsimd.tensor_scalar(
                    out=normed[:], in0=live[i]["r"][j][:], scalar1=live[i]["rstd"][:, j:j + 1],
                    scalar2=live[i]["offset"][:, j:j + 1], op0=MULT, op1=ADD,
                )
                live[i]["normed"].append(normed)

        def turn_back(i):
            live[i]["channels"] = []
            for u in range(2):
                channels = psum1.tile([P, 2, PAIR, P], F32, name=f"channels{u}")
                for e in range(2):
                    t = 2 * u + e
                    for j in range(PAIR):
                        nc.tensor.transpose(channels[:, e, j, :], live[i]["normed"][j][:, t * P:(t + 1) * P], ident[:])
                live[i]["channels"].append(channels)

        def affine(i):
            planes = work.tile([P, PACK, PAIR * P], BF16, name="planes")
            for t in range(PACK):
                nc.scalar.activation(
                    out=planes[:, t, :], in_=live[i]["channels"][t // 2][:, t % 2, :, :].rearrange("p j r -> p (j r)"),
                    func=ACT.Identity, scale=gain_shift[:, 0, t:t + 1], bias=gain_shift[:, 1, t:t + 1],
                )
            live[i]["planes"] = planes

        def weave(i):
            woven = work.tile([P, PAIR * P * PACK], BF16, name="woven", align_bytes=64)
            nc.gpsimd.tensor_scalar(
                out=woven[:].rearrange("p (r t) -> p r t", t=PACK), in0=live[i]["planes"][:].rearrange("p t r -> p r t"),
                scalar1=1.0, scalar2=0.0, op0=MULT, op1=ADD,
            )
            live[i]["woven"] = woven

        def quantise_m(i):
            codes = work.tile([P, PAIR * P], U32, name="m_codes", align_bytes=64)
            scales = work.tile([P, PAIR * P], U8, name="m_scales", align_bytes=64)
            nc.vector.quantize_mx(out=codes[:].bitcast(FP8X4), scales=scales[:], in_=live[i]["woven"][:])
            live[i]["m"] = codes, scales
            live[i]["result"] = work.tile([P, PAIR, F], F32, name="result")

        def expand(i, j, h):
            codes, scales = live[i]["m"]
            tokens = slice(j * P, (j + 1) * P)
            cols = slice(h * BANK, (h + 1) * BANK)
            z = psum2.tile([P, BANK], F32, name="z")
            nc.tensor.matmul_mx(
                out=z[:], lhsT=codes[:, tokens].bitcast(FP8X4), lhsT_scale=scales[:, tokens],
                rhs=w2[:, cols].bitcast(FP8X4), rhs_scale=w2_scales[:, cols], start=True, stop=True,
            )
            nc.vector.tensor_tensor(out=live[i]["result"][:, j, cols], in0=z[:], in1=bias[:, cols], op=ADD)

        def finish(i, j):
            s, h = divmod(i, HALVES)
            result = live[i]["result"]
            pieces = 2 if i == PAIRS - 1 else 1
            width = F // pieces
            for c in range(pieces):
                cols = slice(c * width, (c + 1) * width)
                if i % 4 == 3 and j == 0:
                    nc.vector.tensor_scalar(out=result[:, j, cols], in0=result[:, j, cols], scalar1=0.0, scalar2=None, op0=MAX)
                else:
                    nc.scalar.activation(out=result[:, j, cols], in_=result[:, j, cols], func=ACT.Relu)
                nc.sync.dma_start(
                    out=out[s].rearrange("(p j) f -> p j f", j=ROWS)[:, h * PAIR + j, cols], in_=result[:, j, cols],
                )

        stages = {
            "prepare": prepare, "widen": widen, "turn": turn, "scale": scale, "quantise_ax": quantise_ax,
            "project": project, "residual": residual, "spread": spread, "centre": centre, "normalise": normalise,
            "turn_back": turn_back, "affine": affine, "weave": weave, "quantise_m": quantise_m, "busy": busy,
            "expand_00": lambda i: expand(i, 0, 0), "expand_01": lambda i: expand(i, 0, 1),
            "expand_10": lambda i: expand(i, 1, 0), "expand_11": lambda i: expand(i, 1, 1),
            "finish_0": lambda i: finish(i, 0), "finish_1": lambda i: finish(i, 1),
        }
        text = [(100 * i + delay, place, i) for i in range(PAIRS) for place, (name, delay) in enumerate(DELAYS)]
        for when, place, i in sorted(text):
            stages[DELAYS[place][0]](i)
